import numpy as np
import ml_dtypes


def mxq(x, axis, fmt="e4m3"):
    dtype, down = {"e4m3": (ml_dtypes.float8_e4m3fn, 7), "e5m2": (ml_dtypes.float8_e5m2, 14)}[fmt]
    v = np.moveaxis(np.asarray(x, np.float32).astype(ml_dtypes.bfloat16).astype(np.float64), axis, -1)
    blocks = v.reshape(v.shape[:-1] + (-1, 32))
    amax = np.abs(blocks).max(-1, keepdims=True)
    byte = np.maximum(np.where(amax > 0, np.frexp(amax)[1] - 1 + 127, 0) - down, 1)
    scale = np.exp2(byte - 127.0)
    codes = (blocks / scale).astype(np.float32).astype(dtype).astype(np.float64)
    return np.moveaxis((codes * scale).reshape(v.shape), -1, axis)


WIDE = False


def mx_kscale(k):
    if not WIDE:
        return np.ones(k)
    levels = np.array([10, -10, 5, -5, 0])
    a = np.random.permutation(np.resize(levels, k // 512 * 4)).reshape(k // 512, 4)
    idx = np.arange(k)
    return np.exp2(a[idx // 512, idx % 128 // 32])


BF16 = ml_dtypes.bfloat16


def bf(x):
    return np.asarray(x, np.float32).astype(BF16)


def f64(x):
    return np.asarray(x).astype(np.float64)


B, L, D, DK, DV = 8, 512, 512, 256, 1024


def skew(qe):
    b, l, m = qe.shape
    cat = np.concatenate([np.zeros((b, l, 1)), qe], axis=2)
    return cat.reshape(b, m + 1, l)[:, 1:, :]


def setup_inputs():
    s = mx_kscale(D)
    return {"q": bf(np.random.standard_normal((B, L, DK)) * 1.5),
            "k": bf(np.random.standard_normal((B, L, DK)) * 1.2),
            "inputV": bf(np.random.standard_normal((B, L, D)) * s),
            "Wv": bf(np.random.standard_normal((D, DV)) / np.sqrt(D) / s[:, None]),
            "E": bf(np.random.standard_normal((L, DK)))}


def reference(q, k, inputV, Wv, E):
    v = mxq(f64(inputV), 2, "e4m3") @ mxq(f64(Wv), 0, "e4m3")
    qe = f64(q) @ f64(E).T
    srel = skew(qe)
    qkt = f64(q) @ f64(k).transpose(0, 2, 1)
    sc = (qkt + srel) / np.sqrt(DK)
    e = np.exp(sc - sc.max(-1, keepdims=True))
    return (mxq(e, 2, "e4m3") @ mxq(v, 1, "e4m3")) / e.sum(-1, keepdims=True)

@@ -1,0 +1,312 @@
+from contextlib import ExitStack
+
+import concourse.masks as masks
+import concourse.mybir as mybir
+
+F32 = mybir.dt.float32
+BF16 = mybir.dt.bfloat16
+U32 = mybir.dt.uint32
+U8 = mybir.dt.uint8
+FP8X4 = mybir.dt.float8_e4m3fn_x4
+ADD = mybir.AluOpType.add
+MULT = mybir.AluOpType.mult
+MAX = mybir.AluOpType.max
+EXP = mybir.ActivationFunctionType.Exp
+COPY = mybir.ActivationFunctionType.Copy
+FREE_AXIS = mybir.AxisListType.X
+
+B, L, D, DK, DV = 8, 512, 512, 256, 1024
+P = 128
+TILES = L // P
+BANK = 512
+PACK = 4
+INV_SQRT_DK = 1.0 / 16.0
+PAD = 8
+AHEAD = 3
+N_CAT = 2
+
+FLOPS = 2 * B * (L * D * DV + L * L * DV + 2 * L * L * DK)
+
+
+def pairs(words):
+    return words[:].bitcast(BF16).rearrange("w (c e) -> w c e", e=2)
+
+
+def tile_relativeglobalattention_pa_t_kernel(tc, q, k, inputV, Wv, E, out):
+    nc = tc.nc
+    with ExitStack() as ctx:
+        ctx.enter_context(tc.manual_schedule())
+        const = ctx.enter_context(tc.tile_pool(name="const", bufs=1))
+        rows = ctx.enter_context(tc.tile_pool(name="rows", bufs=2))
+        turned = ctx.enter_context(tc.tile_pool(name="turned", bufs=AHEAD))
+        work = ctx.enter_context(tc.tile_pool(name="work", bufs=2))
+        psum = ctx.enter_context(tc.psum_pool(name="psum", bufs=8))
+
+        q_rows_of, k_rows_of, x_rows_of = {}, {}, {}
+        qT_of, kT_of, x_grouped_of, x_codes_of, x_scales_of = {}, {}, {}, {}, {}
+        v_grouped_of, v_codes_of, v_scales_of = {}, {}, {}
+        s_of, e_rows_of, neg_max_of, row_sum_of, r_inv_of = {}, {}, {}, {}, {}
+        e_grouped_of, e_codes_of, e_scales_of, o_rows_of = {}, {}, {}, {}
+
+        ident_f32 = const.tile([P, P], F32)
+        masks.make_identity(nc, ident_f32[:])
+        ident_bf16 = const.tile([P, P], BF16)
+        masks.make_identity(nc, ident_bf16[:])
+        warm = const.tile([P, 1], F32)
+        nc.vector.memset(warm[:], 0.0)
+        nc.scalar.activation(out=warm[:], in_=warm[:], func=EXP)
+        cats = [const.tile([P, TILES, PAD + L], F32, name="cat%d" % n) for n in range(N_CAT)]
+        for cat in cats:
+            nc.vector.memset(cat[:, :, 0:PAD], 0.0)
+
+        def load_inputs(b):
+            q_rows = rows.tile([P, TILES * DK], BF16)
+            nc.sync.dma_start(out=q_rows[:], in_=q[b].rearrange("(p a) d -> p (a d)", a=TILES))
+            k_rows = rows.tile([P, TILES * DK], BF16)
+            nc.sync.dma_start(out=k_rows[:], in_=k[b].rearrange("(p t) d -> p (t d)", t=TILES))
+            x_rows = rows.tile([P, TILES * D], BF16)
+            nc.sync.dma_start(
+                out=x_rows[:].rearrange("m (t d) -> m t d", t=TILES),
+                in_=inputV[b].rearrange("(t m) d -> m t d", t=TILES),
+            )
+            q_rows_of[b], k_rows_of[b], x_rows_of[b] = q_rows, k_rows, x_rows
+
+        def turn_words(src_rows, first):
+            words = src_rows[:].bitcast(F32)
+            bank = psum.tile([P, BANK], F32, tag="bank")
+            for n in range(4):
+                nc.tensor.transpose(
+                    bank[:, n * P : (n + 1) * P], words[:, (first + n) * P : (first + n + 1) * P], ident_f32[:]
+                )
+            return bank
+
+        def turn_interleaved_rows(src_rows, dst_words):
+            bank = turn_words(src_rows, 0)
+            nc.scalar.copy(
+                out=dst_words[:].rearrange("w (p t) -> w p t", t=4),
+                in_=bank[:].rearrange("w (t p) -> w p t", t=4),
+            )
+
+        def turn_inputs(b):
+            qT = turned.tile([P, L], F32)
+            bank_q = turn_words(q_rows_of[b], 0)
+            nc.scalar.copy(out=qT[:], in_=bank_q[:])
+            kT = turned.tile([P, L], F32)
+            turn_interleaved_rows(k_rows_of[b], kT)
+            x_grouped = work.tile([P, L * PACK], BF16, align_bytes=64)
+            grouped_words = x_grouped[:].bitcast(F32)
+            for h in range(2):
+                bank_x = turn_words(x_rows_of[b], 4 * h)
+                nc.scalar.copy(
+                    out=grouped_words[:, h * BANK : (h + 1) * BANK].rearrange("w (t m u) -> w t m u", t=2, u=2),
+                    in_=bank_x[:].rearrange("w (t u m) -> w t m u", t=2, u=2),
+                )
+            qT_of[b], kT_of[b], x_grouped_of[b] = qT, kT, x_grouped
+
+        def quantise_x(b):
+            x_codes = work.tile([P, L], U32, align_bytes=64)
+            x_scales = work.tile([P, L], U8, align_bytes=64)
+            nc.vector.quantize_mx(out=x_codes[:].bitcast(FP8X4), scales=x_scales[:], in_=x_grouped_of[b][:])
+            x_codes_of[b], x_scales_of[b] = x_codes, x_scales
+
+        def new_values(b):
+            v_grouped = work.tile([P, DV * PACK], BF16, align_bytes=64)
+            v_codes = work.tile([P, DV], U32, align_bytes=64)
+            v_scales = work.tile([P, DV], U8, align_bytes=64)
+            v_grouped_of[b], v_codes_of[b], v_scales_of[b] = v_grouped, v_codes, v_scales
+
+        def project_values(b, c):
+            cols = slice(c * P, (c + 1) * P)
+            bank_v = psum.tile([P, BANK], F32, tag="bank")
+            for t in range(TILES):
+                keys = slice(t * P, (t + 1) * P)
+                nc.tensor.matmul_mx(
+                    out=bank_v[:, keys],
+                    lhsT=x_codes_of[b][:, keys].bitcast(FP8X4),
+                    lhsT_scale=x_scales_of[b][:, keys],
+                    rhs=wv_codes[:, cols].bitcast(FP8X4),
+                    rhs_scale=wv_scales[:, cols],
+                    start=True,
+                    stop=True,
+                )
+            nc.vector.tensor_copy(
+                out=v_grouped_of[b][:, c * BANK : (c + 1) * BANK].rearrange("p (n t) -> p n t", t=PACK),
+                in_=bank_v[:].rearrange("p (t n) -> p n t", t=PACK),
+            )
+
+        def quantise_v(b, h):
+            half = slice(h * BANK, (h + 1) * BANK)
+            nc.vector.quantize_mx(
+                out=v_codes_of[b][:, half].bitcast(FP8X4),
+                scales=v_scales_of[b][:, half],
+                in_=v_grouped_of[b][:, h * BANK * PACK : (h + 1) * BANK * PACK],
+            )
+
+        def plain_logits(b, a, keysT):
+            bank = psum.tile([P, BANK], F32, tag="bank")
+            for e in range(2):
+                nc.tensor.matmul(
+                    bank[:],
+                    lhsT=pairs(qT_of[b])[:, a * P : (a + 1) * P, e],
+                    rhs=pairs(keysT)[:, :, e],
+                    start=(e == 0),
+                    stop=(e == 1),
+                )
+            return bank
+
+        def relative_logits(b, a):
+            bank_qe = plain_logits(b, a, ET)
+            nc.scalar.mul(out=cats[b % N_CAT][:, a, PAD : PAD + L], in_=bank_qe[:], mul=INV_SQRT_DK)
+
+        def skew(b):
+            flat = out[b].rearrange("l d -> (l d)")
+            nc.sync.dma_start(
+                out=flat[0 : L * (L + 1)].rearrange("(p a c) -> p a c", a=TILES, c=L + 1),
+                in_=cats[b % N_CAT][:, :, PAD - 1 : PAD + L],
+            )
+            s = turned.tile([P, TILES * L], F32)
+            nc.gpsimd.dma_start(out=s[:], in_=flat[L : L + L * L].rearrange("(p x) -> p x", p=P))
+            s_of[b] = s
+
+        def new_softmax(b):
+            e_rows = work.tile([P, TILES * L], BF16)
+            neg_max = work.tile([P, TILES], F32)
+            row_sum = work.tile([P, TILES], F32)
+            e_rows_of[b], neg_max_of[b], row_sum_of[b] = e_rows, neg_max, row_sum
+
+        def add_and_max(b, a):
+            bank_qk = plain_logits(b, a, kT_of[b])
+            s_a = s_of[b][:, a * L : (a + 1) * L]
+            nc.vector.scalar_tensor_tensor(
+                out=s_a, in0=bank_qk[:], scalar=INV_SQRT_DK, in1=s_a, op0=MULT, op1=ADD
+            )
+            nc.vector.tensor_reduce(
+                out=neg_max_of[b][:, a : a + 1], in_=s_a, axis=FREE_AXIS, op=MAX, negate=True
+            )
+
+        def exponentials(b, a):
+            nc.scalar.activation(
+                out=e_rows_of[b][:, a * L : (a + 1) * L],
+                in_=s_of[b][:, a * L : (a + 1) * L],
+                func=EXP,
+                bias=neg_max_of[b][:, a : a + 1],
+                scale=1.0,
+                accum_out=row_sum_of[b][:, a : a + 1],
+            )
+
+        def invert_row_sums(b):
+            r_inv = work.tile([P, TILES], F32)
+            nc.vector.reciprocal(out=r_inv[:], in_=row_sum_of[b][:])
+            r_inv_of[b] = r_inv
+
+        def turn_e(b):
+            e_grouped = work.tile([P, L * PACK], BF16, align_bytes=64)
+            for h in range(2):
+                bank_e = psum.tile([P, 2 * BANK], BF16, tag="bank")
+                for n in range(2 * TILES):
+                    first = (2 * TILES * h + n) * P
+                    nc.tensor.transpose(
+                        bank_e[:, n * P : (n + 1) * P], e_rows_of[b][:, first : first + P], ident_bf16[:]
+                    )
+                nc.scalar.copy(
+                    out=e_grouped[:, h * 2 * BANK : (h + 1) * 2 * BANK].rearrange("p (a i t) -> p a i t", a=2, t=PACK),
+                    in_=bank_e[:].rearrange("p (a t i) -> p a i t", a=2, t=PACK),
+                )
+            e_grouped_of[b] = e_grouped
+
+        def quantise_e(b):
+            e_codes = work.tile([P, L], U32, align_bytes=64)
+            e_scales = work.tile([P, L], U8, align_bytes=64)
+            nc.vector.quantize_mx(out=e_codes[:].bitcast(FP8X4), scales=e_scales[:], in_=e_grouped_of[b][:])
+            e_codes_of[b], e_scales_of[b] = e_codes, e_scales
+
+        def attend(b, g):
+            if g == 0:
+                o_rows = work.tile([P, TILES * DV], F32)
+                o_rows_of[b] = o_rows
+            for n in range(4):
+                a, h = 2 * g + n // 2, n % 2
+                queries = slice(a * P, (a + 1) * P)
+                half = slice(h * BANK, (h + 1) * BANK)
+                bank_o = psum.tile([P, BANK], F32, tag="bank")
+                nc.tensor.matmul_mx(
+                    out=bank_o[:],
+                    lhsT=e_codes_of[b][:, queries].bitcast(FP8X4),
+                    lhsT_scale=e_scales_of[b][:, queries],
+                    rhs=v_codes_of[b][:, half].bitcast(FP8X4),
+                    rhs_scale=v_scales_of[b][:, half],
+                    start=True,
+                    stop=True,
+                )
+                o_part = o_rows_of[b][:, a * DV + h * BANK : a * DV + (h + 1) * BANK]
+                r_inv_a = r_inv_of[b][:, a : a + 1]
+                if n < 3:
+                    nc.scalar.activation(out=o_part, in_=bank_o[:], func=COPY, scale=r_inv_a)
+                else:
+                    nc.vector.tensor_scalar_mul(out=o_part, in0=bank_o[:], scalar1=r_inv_a)
+            part = slice(g * 2 * DV, (g + 1) * 2 * DV)
+            nc.sync.dma_start(
+                out=out[b].rearrange("(p a) d -> p (a d)", a=TILES)[:, part], in_=o_rows_of[b][:, part]
+            )
+
+        e_table_rows = const.tile([P, TILES * DK], BF16)
+        nc.sync.dma_start(out=e_table_rows[:], in_=E.rearrange("(p t) d -> p (t d)", t=TILES))
+        load_inputs(0)
+        wv_rows = const.tile([P, PACK * DV], BF16)
+        nc.sync.dma_start(
+            out=wv_rows[:].rearrange("w (u x) -> w u x", u=2),
+            in_=Wv.rearrange("(u w e) n -> w u (e n)", u=2, e=2),
+        )
+        ET = const.tile([P, L], F32)
+        turn_interleaved_rows(e_table_rows, ET)
+        wv_grouped = const.tile([P, DV * PACK], BF16, align_bytes=64)
+        nc.vector.tensor_copy(
+            out=wv_grouped[:].rearrange("w (n t) -> w n t", t=PACK),
+            in_=wv_rows[:].rearrange("w (t n) -> w n t", t=PACK),
+        )
+        wv_codes = const.tile([P, DV], U32, align_bytes=64)
+        wv_scales = const.tile([P, DV], U8, align_bytes=64)
+        nc.vector.quantize_mx(out=wv_codes[:].bitcast(FP8X4), scales=wv_scales[:], in_=wv_grouped[:])
+
+        def live(b):
+            return 0 <= b < B
+
+        for i in range(-AHEAD, B):
+            if live(i + AHEAD + 1):
+                load_inputs(i + AHEAD + 1)
+            if live(i + 1):
+                new_values(i + 1)
+                for c in range(0, 4):
+                    project_values(i + 1, c)
+            if live(i + 2):
+                quantise_x(i + 2)
+            if live(i + 1):
+                quantise_v(i + 1, 0)
+            if live(i):
+                turn_e(i)
+            if live(i + AHEAD):
+                turn_inputs(i + AHEAD)
+            if live(i):
+                quantise_e(i)
+            if live(i + 1):
+                for c in range(4, 8):
+                    project_values(i + 1, c)
+            if live(i):
+                attend(i, 0)
+            if live(i + 1):
+                quantise_v(i + 1, 1)
+            if live(i):
+                attend(i, 1)
+            if live(i + 1):
+                new_softmax(i + 1)
+            for a in range(TILES):
+                if live(i + 1):
+                    add_and_max(i + 1, a)
+                if live(i + AHEAD):
+                    relative_logits(i + AHEAD, a)
+                if live(i + 1):
+                    exponentials(i + 1, a)
+            if live(i + 1):
+                invert_row_sums(i + 1)
+            if live(i + AHEAD):
+                skew(i + AHEAD)

@@ -22,7 +22,9 @@ BANK = 512
 PACK = 4
 INV_SQRT_DK = 1.0 / 16.0
 PAD = 8
+BANKS = 8
 AHEAD = 3
+LOADS_AHEAD = 2
 N_CAT = 2
 
 FLOPS = 2 * B * (L * D * DV + L * L * DV + 2 * L * L * DK)
@@ -37,10 +39,10 @@ def tile_relativeglobalattention_pa_t_kernel(tc, q, k, inputV, Wv, E, out):
     with ExitStack() as ctx:
         ctx.enter_context(tc.manual_schedule())
         const = ctx.enter_context(tc.tile_pool(name="const", bufs=1))
-        rows = ctx.enter_context(tc.tile_pool(name="rows", bufs=2))
+        rows = ctx.enter_context(tc.tile_pool(name="rows", bufs=LOADS_AHEAD + 2))
         turned = ctx.enter_context(tc.tile_pool(name="turned", bufs=AHEAD))
         work = ctx.enter_context(tc.tile_pool(name="work", bufs=2))
-        psum = ctx.enter_context(tc.psum_pool(name="psum", bufs=8))
+        psum = ctx.enter_context(tc.psum_pool(name="psum", bufs=BANKS))
 
         q_rows_of, k_rows_of, x_rows_of = {}, {}, {}
         qT_of, kT_of, x_grouped_of, x_codes_of, x_scales_of = {}, {}, {}, {}, {}
@@ -58,6 +60,9 @@ def tile_relativeglobalattention_pa_t_kernel(tc, q, k, inputV, Wv, E, out):
         cats = [const.tile([P, TILES, PAD + L], F32, name="cat%d" % n) for n in range(N_CAT)]
         for cat in cats:
             nc.vector.memset(cat[:, :, 0:PAD], 0.0)
+
+        def live(b):
+            return 0 <= b < B
 
         def load_inputs(b):
             q_rows = rows.tile([P, TILES * DK], BF16)
@@ -87,10 +92,13 @@ def tile_relativeglobalattention_pa_t_kernel(tc, q, k, inputV, Wv, E, out):
                 in_=bank[:].rearrange("w (t p) -> w p t", t=4),
             )
 
-        def turn_inputs(b):
+        def turn_q(b):
             qT = turned.tile([P, L], F32)
             bank_q = turn_words(q_rows_of[b], 0)
             nc.scalar.copy(out=qT[:], in_=bank_q[:])
+            qT_of[b] = qT
+
+        def turn_kx(b):
             kT = turned.tile([P, L], F32)
             turn_interleaved_rows(k_rows_of[b], kT)
             x_grouped = work.tile([P, L * PACK], BF16, align_bytes=64)
@@ -101,7 +109,7 @@ def tile_relativeglobalattention_pa_t_kernel(tc, q, k, inputV, Wv, E, out):
                     out=grouped_words[:, h * BANK : (h + 1) * BANK].rearrange("w (t m u) -> w t m u", t=2, u=2),
                     in_=bank_x[:].rearrange("w (t u m) -> w t m u", t=2, u=2),
                 )
-            qT_of[b], kT_of[b], x_grouped_of[b] = qT, kT, x_grouped
+            kT_of[b], x_grouped_of[b] = kT, x_grouped
 
         def quantise_x(b):
             x_codes = work.tile([P, L], U32, align_bytes=64)
@@ -111,8 +119,8 @@ def tile_relativeglobalattention_pa_t_kernel(tc, q, k, inputV, Wv, E, out):
 
         def new_values(b):
             v_grouped = work.tile([P, DV * PACK], BF16, align_bytes=64)
-            v_codes = work.tile([P, DV], U32, align_bytes=64)
-            v_scales = work.tile([P, DV], U8, align_bytes=64)
+            v_codes = work.tile([P, DV], U32, align_bytes=64, bufs=3)
+            v_scales = work.tile([P, DV], U8, align_bytes=64, bufs=3)
             v_grouped_of[b], v_codes_of[b], v_scales_of[b] = v_grouped, v_codes, v_scales
 
         def project_values(b, c):
@@ -129,7 +137,8 @@ def tile_relativeglobalattention_pa_t_kernel(tc, q, k, inputV, Wv, E, out):
                     start=True,
                     stop=True,
                 )
-            nc.vector.tensor_copy(
+            copy_out = nc.scalar.copy if (c % 2 == 1 and not live(b - 2)) else nc.vector.tensor_copy
+            copy_out(
                 out=v_grouped_of[b][:, c * BANK : (c + 1) * BANK].rearrange("p (n t) -> p n t", t=PACK),
                 in_=bank_v[:].rearrange("p (t n) -> p n t", t=PACK),
             )
@@ -174,14 +183,20 @@ def tile_relativeglobalattention_pa_t_kernel(tc, q, k, inputV, Wv, E, out):
             row_sum = work.tile([P, TILES], F32)
             e_rows_of[b], neg_max_of[b], row_sum_of[b] = e_rows, neg_max, row_sum
 
-        def add_and_max(b, a):
+        def add_logits(b, a):
             bank_qk = plain_logits(b, a, kT_of[b])
             s_a = s_of[b][:, a * L : (a + 1) * L]
             nc.vector.scalar_tensor_tensor(
                 out=s_a, in0=bank_qk[:], scalar=INV_SQRT_DK, in1=s_a, op0=MULT, op1=ADD
             )
+
+        def row_max(b, a):
             nc.vector.tensor_reduce(
-                out=neg_max_of[b][:, a : a + 1], in_=s_a, axis=FREE_AXIS, op=MAX, negate=True
+                out=neg_max_of[b][:, a : a + 1],
+                in_=s_of[b][:, a * L : (a + 1) * L],
+                axis=FREE_AXIS,
+                op=MAX,
+                negate=True,
             )
 
         def exponentials(b, a):
@@ -208,7 +223,8 @@ def tile_relativeglobalattention_pa_t_kernel(tc, q, k, inputV, Wv, E, out):
                     nc.tensor.transpose(
                         bank_e[:, n * P : (n + 1) * P], e_rows_of[b][:, first : first + P], ident_bf16[:]
                     )
-                nc.scalar.copy(
+                copy_out = nc.vector.tensor_copy if h == 0 else nc.scalar.copy
+                copy_out(
                     out=e_grouped[:, h * 2 * BANK : (h + 1) * 2 * BANK].rearrange("p (a i t) -> p a i t", a=2, t=PACK),
                     in_=bank_e[:].rearrange("p (a t i) -> p a i t", a=2, t=PACK),
                 )
@@ -220,34 +236,34 @@ def tile_relativeglobalattention_pa_t_kernel(tc, q, k, inputV, Wv, E, out):
             nc.vector.quantize_mx(out=e_codes[:].bitcast(FP8X4), scales=e_scales[:], in_=e_grouped_of[b][:])
             e_codes_of[b], e_scales_of[b] = e_codes, e_scales
 
-        def attend(b, g):
-            if g == 0:
+        def attend(b, n):
+            if n == 0:
                 o_rows = work.tile([P, TILES * DV], F32)
                 o_rows_of[b] = o_rows
-            for n in range(4):
-                a, h = 2 * g + n // 2, n % 2
-                queries = slice(a * P, (a + 1) * P)
-                half = slice(h * BANK, (h + 1) * BANK)
-                bank_o = psum.tile([P, BANK], F32, tag="bank")
-                nc.tensor.matmul_mx(
-                    out=bank_o[:],
-                    lhsT=e_codes_of[b][:, queries].bitcast(FP8X4),
-                    lhsT_scale=e_scales_of[b][:, queries],
-                    rhs=v_codes_of[b][:, half].bitcast(FP8X4),
-                    rhs_scale=v_scales_of[b][:, half],
-                    start=True,
-                    stop=True,
-                )
-                o_part = o_rows_of[b][:, a * DV + h * BANK : a * DV + (h + 1) * BANK]
-                r_inv_a = r_inv_of[b][:, a : a + 1]
-                if n < 3:
-                    nc.scalar.activation(out=o_part, in_=bank_o[:], func=COPY, scale=r_inv_a)
-                else:
-                    nc.vector.tensor_scalar_mul(out=o_part, in0=bank_o[:], scalar1=r_inv_a)
-            part = slice(g * 2 * DV, (g + 1) * 2 * DV)
-            nc.sync.dma_start(
-                out=out[b].rearrange("(p a) d -> p (a d)", a=TILES)[:, part], in_=o_rows_of[b][:, part]
+            a, h = n // 2, n % 2
+            queries = slice(a * P, (a + 1) * P)
+            half = slice(h * BANK, (h + 1) * BANK)
+            bank_o = psum.tile([P, BANK], F32, tag="bank")
+            nc.tensor.matmul_mx(
+                out=bank_o[:],
+                lhsT=e_codes_of[b][:, queries].bitcast(FP8X4),
+                lhsT_scale=e_scales_of[b][:, queries],
+                rhs=v_codes_of[b][:, half].bitcast(FP8X4),
+                rhs_scale=v_scales_of[b][:, half],
+                start=True,
+                stop=True,
             )
+            o_part = o_rows_of[b][:, a * DV + h * BANK : a * DV + (h + 1) * BANK]
+            r_inv_a = r_inv_of[b][:, a : a + 1]
+            if n % 2 == 0 or live(b + 2):
+                nc.scalar.activation(out=o_part, in_=bank_o[:], func=COPY, scale=r_inv_a)
+            else:
+                nc.vector.tensor_scalar_mul(out=o_part, in0=bank_o[:], scalar1=r_inv_a)
+            if h == 1:
+                part = slice(a * DV, (a + 1) * DV)
+                nc.sync.dma_start(
+                    out=out[b].rearrange("(p a) d -> p (a d)", a=TILES)[:, part], in_=o_rows_of[b][:, part]
+                )
 
         e_table_rows = const.tile([P, TILES * DK], BF16)
         nc.sync.dma_start(out=e_table_rows[:], in_=E.rearrange("(p t) d -> p (t d)", t=TILES))
@@ -257,6 +273,8 @@ def tile_relativeglobalattention_pa_t_kernel(tc, q, k, inputV, Wv, E, out):
             out=wv_rows[:].rearrange("w (u x) -> w u x", u=2),
             in_=Wv.rearrange("(u w e) n -> w u (e n)", u=2, e=2),
         )
+        for b in range(1, LOADS_AHEAD):
+            load_inputs(b)
         ET = const.tile([P, L], F32)
         turn_interleaved_rows(e_table_rows, ET)
         wv_grouped = const.tile([P, DV * PACK], BF16, align_bytes=64)
@@ -268,45 +286,44 @@ def tile_relativeglobalattention_pa_t_kernel(tc, q, k, inputV, Wv, E, out):
         wv_scales = const.tile([P, DV], U8, align_bytes=64)
         nc.vector.quantize_mx(out=wv_codes[:].bitcast(FP8X4), scales=wv_scales[:], in_=wv_grouped[:])
 
-        def live(b):
-            return 0 <= b < B
+        for i in range(-AHEAD, B + 1):
+            if live(i + AHEAD + LOADS_AHEAD):
+                load_inputs(i + AHEAD + LOADS_AHEAD)
 
-        for i in range(-AHEAD, B):
-            if live(i + AHEAD + 1):
-                load_inputs(i + AHEAD + 1)
             if live(i + 1):
                 new_values(i + 1)
-                for c in range(0, 4):
-                    project_values(i + 1, c)
+            for n in range(BANKS):
+                if live(i + 1):
+                    project_values(i + 1, n)
+                    if n == BANKS // 2 + 1:
+                        quantise_v(i + 1, 0)
+                if live(i - 1):
+                    attend(i - 1, n)
             if live(i + 2):
                 quantise_x(i + 2)
             if live(i + 1):
-                quantise_v(i + 1, 0)
+                quantise_v(i + 1, 1)
+
+            if live(i + AHEAD):
+                turn_q(i + AHEAD)
             if live(i):
                 turn_e(i)
             if live(i + AHEAD):
-                turn_inputs(i + AHEAD)
-            if live(i):
-                quantise_e(i)
-            if live(i + 1):
-                for c in range(4, 8):
-                    project_values(i + 1, c)
-            if live(i):
-                attend(i, 0)
-            if live(i + 1):
-                quantise_v(i + 1, 1)
-            if live(i):
-                attend(i, 1)
+                turn_kx(i + AHEAD)
+
             if live(i + 1):
                 new_softmax(i + 1)
-            for a in range(TILES):
-                if live(i + 1):
-                    add_and_max(i + 1, a)
-                if live(i + AHEAD):
-                    relative_logits(i + AHEAD, a)
-                if live(i + 1):
-                    exponentials(i + 1, a)
-            if live(i + 1):
-                invert_row_sums(i + 1)
+            for step in range(TILES + 1):
+                if live(i + 1) and step < TILES:
+                    add_logits(i + 1, step)
+                if live(i + 1) and step > 0:
+                    row_max(i + 1, step - 1)
+                if live(i + AHEAD) and step > 0:
+                    relative_logits(i + AHEAD, step - 1)
+                if live(i + 1) and step > 0:
+                    exponentials(i + 1, step - 1)
+                if live(i) and step == 1:
+                    invert_row_sums(i)
+                    quantise_e(i)
             if live(i + AHEAD):
                 skew(i + AHEAD)

@@ -21,7 +21,6 @@ TILES = L // P
 BANK = 512
 PACK = 4
 INV_SQRT_DK = 1.0 / 16.0
-PAD = 8
 BANKS = 8
 AHEAD = 3
 LOADS_AHEAD = 2
@@ -57,9 +56,11 @@ def tile_relativeglobalattention_pa_t_kernel(tc, q, k, inputV, Wv, E, out):
         warm = const.tile([P, 1], F32)
         nc.vector.memset(warm[:], 0.0)
         nc.scalar.activation(out=warm[:], in_=warm[:], func=EXP)
-        cats = [const.tile([P, TILES, PAD + L], F32, name="cat%d" % n) for n in range(N_CAT)]
+        zeros = const.tile([P, TILES, 1], F32)
+        nc.vector.memset(zeros[:], 0.0)
+        cats = [const.tile([P, TILES, 1 + L], F32, name="cat%d" % n) for n in range(N_CAT)]
         for cat in cats:
-            nc.vector.memset(cat[:, :, 0:PAD], 0.0)
+            nc.scalar.copy(out=cat[:, :, 0:1], in_=zeros[:])
 
         def live(b):
             return 0 <= b < B
@@ -165,13 +166,13 @@ def tile_relativeglobalattention_pa_t_kernel(tc, q, k, inputV, Wv, E, out):
 
         def relative_logits(b, a):
             bank_qe = plain_logits(b, a, ET)
-            nc.scalar.mul(out=cats[b % N_CAT][:, a, PAD : PAD + L], in_=bank_qe[:], mul=INV_SQRT_DK)
+            nc.scalar.mul(out=cats[b % N_CAT][:, a, 1 : 1 + L], in_=bank_qe[:], mul=INV_SQRT_DK)
 
         def skew(b):
             flat = out[b].rearrange("l d -> (l d)")
             nc.sync.dma_start(
-                out=flat[0 : L * (L + 1)].rearrange("(p a c) -> p a c", a=TILES, c=L + 1),
-                in_=cats[b % N_CAT][:, :, PAD - 1 : PAD + L],
+                out=flat[0 : L * (L + 1)].rearrange("(p x) -> p x", p=P),
+                in_=cats[b % N_CAT][:].rearrange("p a c -> p (a c)"),
             )
             s = turned.tile([P, TILES * L], F32)
             nc.gpsimd.dma_start(out=s[:], in_=flat[L : L + L * L].rearrange("(p x) -> p x", p=P))

@@ -71,10 +71,7 @@ def tile_relativeglobalattention_pa_t_kernel(tc, q, k, inputV, Wv, E, out):
             k_rows = rows.tile([P, TILES * DK], BF16)
             nc.sync.dma_start(out=k_rows[:], in_=k[b].rearrange("(p t) d -> p (t d)", t=TILES))
             x_rows = rows.tile([P, TILES * D], BF16)
-            nc.sync.dma_start(
-                out=x_rows[:].rearrange("m (t d) -> m t d", t=TILES),
-                in_=inputV[b].rearrange("(t m) d -> m t d", t=TILES),
-            )
+            nc.sync.dma_start(out=x_rows[:], in_=inputV[b].rearrange("(m t) d -> m (t d)", t=TILES))
             q_rows_of[b], k_rows_of[b], x_rows_of[b] = q_rows, k_rows, x_rows
 
         def turn_words(src_rows, first):
@@ -103,13 +100,10 @@ def tile_relativeglobalattention_pa_t_kernel(tc, q, k, inputV, Wv, E, out):
             kT = turned.tile([P, L], F32)
             turn_interleaved_rows(k_rows_of[b], kT)
             x_grouped = work.tile([P, L * PACK], BF16, align_bytes=64)
-            grouped_words = x_grouped[:].bitcast(F32)
+            grouped_words = x_grouped[:].bitcast(F32).rearrange("w (m h c) -> w m h c", h=2, c=4)
             for h in range(2):
                 bank_x = turn_words(x_rows_of[b], 4 * h)
-                nc.scalar.copy(
-                    out=grouped_words[:, h * BANK : (h + 1) * BANK].rearrange("w (t m u) -> w t m u", t=2, u=2),
-                    in_=bank_x[:].rearrange("w (t u m) -> w t m u", t=2, u=2),
-                )
+                nc.scalar.copy(out=grouped_words[:, :, h, :], in_=bank_x[:].rearrange("w (c m) -> w m c", c=4))
             kT_of[b], x_grouped_of[b] = kT, x_grouped
 
         def quantise_x(b):

@@ -51,8 +51,6 @@ def tile_relativeglobalattention_pa_t_kernel(tc, q, k, inputV, Wv, E, out):
 
         ident_f32 = const.tile([P, P], F32)
         masks.make_identity(nc, ident_f32[:])
-        ident_bf16 = const.tile([P, P], BF16)
-        masks.make_identity(nc, ident_bf16[:])
         warm = const.tile([P, 1], F32)
         nc.vector.memset(warm[:], 0.0)
         nc.scalar.activation(out=warm[:], in_=warm[:], func=EXP)
@@ -74,17 +72,17 @@ def tile_relativeglobalattention_pa_t_kernel(tc, q, k, inputV, Wv, E, out):
             nc.sync.dma_start(out=x_rows[:], in_=inputV[b].rearrange("(m t) d -> m (t d)", t=TILES))
             q_rows_of[b], k_rows_of[b], x_rows_of[b] = q_rows, k_rows, x_rows
 
-        def turn_words(src_rows, first):
+        def turn_words(src_rows, blocks):
             words = src_rows[:].bitcast(F32)
             bank = psum.tile([P, BANK], F32, tag="bank")
-            for n in range(4):
+            for n, block in enumerate(blocks):
                 nc.tensor.transpose(
-                    bank[:, n * P : (n + 1) * P], words[:, (first + n) * P : (first + n + 1) * P], ident_f32[:]
+                    bank[:, n * P : (n + 1) * P], words[:, block * P : (block + 1) * P], ident_f32[:]
                 )
             return bank
 
         def turn_interleaved_rows(src_rows, dst_words):
-            bank = turn_words(src_rows, 0)
+            bank = turn_words(src_rows, range(4))
             nc.scalar.copy(
                 out=dst_words[:].rearrange("w (p t) -> w p t", t=4),
                 in_=bank[:].rearrange("w (t p) -> w p t", t=4),
@@ -92,7 +90,7 @@ def tile_relativeglobalattention_pa_t_kernel(tc, q, k, inputV, Wv, E, out):
 
         def turn_q(b):
             qT = turned.tile([P, L], F32)
-            bank_q = turn_words(q_rows_of[b], 0)
+            bank_q = turn_words(q_rows_of[b], range(4))
             nc.scalar.copy(out=qT[:], in_=bank_q[:])
             qT_of[b] = qT
 
@@ -100,10 +98,12 @@ def tile_relativeglobalattention_pa_t_kernel(tc, q, k, inputV, Wv, E, out):
             kT = turned.tile([P, L], F32)
             turn_interleaved_rows(k_rows_of[b], kT)
             x_grouped = work.tile([P, L * PACK], BF16, align_bytes=64)
-            grouped_words = x_grouped[:].bitcast(F32).rearrange("w (m h c) -> w m h c", h=2, c=4)
-            for h in range(2):
-                bank_x = turn_words(x_rows_of[b], 4 * h)
-                nc.scalar.copy(out=grouped_words[:, :, h, :], in_=bank_x[:].rearrange("w (c m) -> w m c", c=4))
+            grouped_words = x_grouped[:].bitcast(F32).rearrange("w (g f m x) -> w g f m x", g=2, f=2, x=4)
+            for f in range(2):
+                bank_x = turn_words(x_rows_of[b], [2 * (2 * s + f) + u for s in range(2) for u in range(2)])
+                nc.scalar.copy(
+                    out=grouped_words[:, :, f, :, :], in_=bank_x[:].rearrange("w (x g m) -> w g m x", x=4, g=2)
+                )
             kT_of[b], x_grouped_of[b] = kT, x_grouped
 
         def quantise_x(b):
@@ -211,17 +211,13 @@ def tile_relativeglobalattention_pa_t_kernel(tc, q, k, inputV, Wv, E, out):
 
         def turn_e(b):
             e_grouped = work.tile([P, L * PACK], BF16, align_bytes=64)
+            grouped_words = e_grouped[:].bitcast(F32)
             for h in range(2):
-                bank_e = psum.tile([P, 2 * BANK], BF16, tag="bank")
-                for n in range(2 * TILES):
-                    first = (2 * TILES * h + n) * P
-                    nc.tensor.transpose(
-                        bank_e[:, n * P : (n + 1) * P], e_rows_of[b][:, first : first + P], ident_bf16[:]
-                    )
+                bank_e = turn_words(e_rows_of[b], range(4 * h, 4 * h + 4))
                 copy_out = nc.vector.tensor_copy if h == 0 else nc.scalar.copy
                 copy_out(
-                    out=e_grouped[:, h * 2 * BANK : (h + 1) * 2 * BANK].rearrange("p (a i t) -> p a i t", a=2, t=PACK),
-                    in_=bank_e[:].rearrange("p (a t i) -> p a i t", a=2, t=PACK),
+                    out=grouped_words[:, h * BANK : (h + 1) * BANK].rearrange("p (a i u) -> p a i u", a=2, u=2),
+                    in_=bank_e[:].rearrange("p (a u i) -> p a i u", a=2, u=2),
                 )
             e_grouped_of[b] = e_grouped
 

@@ -63,14 +63,25 @@ def tile_relativeglobalattention_pa_t_kernel(tc, q, k, inputV, Wv, E, out):
         def live(b):
             return 0 <= b < B
 
-        def load_inputs(b):
+        def load_q(b):
             q_rows = rows.tile([P, TILES * DK], BF16)
             nc.sync.dma_start(out=q_rows[:], in_=q[b].rearrange("(p a) d -> p (a d)", a=TILES))
+            q_rows_of[b] = q_rows
+
+        def load_k(b):
             k_rows = rows.tile([P, TILES * DK], BF16)
             nc.sync.dma_start(out=k_rows[:], in_=k[b].rearrange("(p t) d -> p (t d)", t=TILES))
+            k_rows_of[b] = k_rows
+
+        def load_x(b):
             x_rows = rows.tile([P, TILES * D], BF16)
             nc.sync.dma_start(out=x_rows[:], in_=inputV[b].rearrange("(m t) d -> m (t d)", t=TILES))
-            q_rows_of[b], k_rows_of[b], x_rows_of[b] = q_rows, k_rows, x_rows
+            x_rows_of[b] = x_rows
+
+        def load_inputs(b):
+            load_q(b)
+            load_x(b)
+            load_k(b)
 
         def turn_words(src_rows, blocks):
             words = src_rows[:].bitcast(F32)
@@ -81,30 +92,34 @@ def tile_relativeglobalattention_pa_t_kernel(tc, q, k, inputV, Wv, E, out):
                 )
             return bank
 
-        def turn_interleaved_rows(src_rows, dst_words):
+        def turn_interleaved_rows(src_rows, dst_words, copy_out=nc.scalar.copy):
             bank = turn_words(src_rows, range(4))
-            nc.scalar.copy(
+            copy_out(
                 out=dst_words[:].rearrange("w (p t) -> w p t", t=4),
                 in_=bank[:].rearrange("w (t p) -> w p t", t=4),
             )
 
-        def turn_q(b):
+        def turn_q(b, copy_out=nc.scalar.copy):
             qT = turned.tile([P, L], F32)
             bank_q = turn_words(q_rows_of[b], range(4))
-            nc.scalar.copy(out=qT[:], in_=bank_q[:])
+            copy_out(out=qT[:], in_=bank_q[:])
             qT_of[b] = qT
 
-        def turn_kx(b):
+        def turn_k(b, copy_out=nc.scalar.copy):
             kT = turned.tile([P, L], F32)
-            turn_interleaved_rows(k_rows_of[b], kT)
+            turn_interleaved_rows(k_rows_of[b], kT, copy_out)
+            kT_of[b] = kT
+
+        def turn_x(b, copies=None):
             x_grouped = work.tile([P, L * PACK], BF16, align_bytes=64)
-            grouped_words = x_grouped[:].bitcast(F32).rearrange("w (g f m x) -> w g f m x", g=2, f=2, x=4)
+            grouped_words = x_grouped[:].bitcast(F32).rearrange("w (f g m x) -> w f g m x", f=2, g=2, x=4)
             for f in range(2):
                 bank_x = turn_words(x_rows_of[b], [2 * (2 * s + f) + u for s in range(2) for u in range(2)])
-                nc.scalar.copy(
-                    out=grouped_words[:, :, f, :, :], in_=bank_x[:].rearrange("w (x g m) -> w g m x", x=4, g=2)
+                copy_out = copies[f] if copies else nc.scalar.copy
+                copy_out(
+                    out=grouped_words[:, f, :, :, :], in_=bank_x[:].rearrange("w (x g m) -> w g m x", x=4, g=2)
                 )
-            kT_of[b], x_grouped_of[b] = kT, x_grouped
+            x_grouped_of[b] = x_grouped
 
         def quantise_x(b):
             x_codes = work.tile([P, L], U32, align_bytes=64)
@@ -114,17 +129,18 @@ def tile_relativeglobalattention_pa_t_kernel(tc, q, k, inputV, Wv, E, out):
 
         def new_values(b):
             v_grouped = work.tile([P, DV * PACK], BF16, align_bytes=64)
-            v_codes = work.tile([P, DV], U32, align_bytes=64, bufs=3)
-            v_scales = work.tile([P, DV], U8, align_bytes=64, bufs=3)
+            v_codes = work.tile([P, DV], U32, align_bytes=64, bufs=4)
+            v_scales = work.tile([P, DV], U8, align_bytes=64, bufs=4)
             v_grouped_of[b], v_codes_of[b], v_scales_of[b] = v_grouped, v_codes, v_scales
 
-        def project_values(b, c):
+        def project_values(b, c, on_scalar):
             cols = slice(c * P, (c + 1) * P)
             bank_v = psum.tile([P, BANK], F32, tag="bank")
             for t in range(TILES):
-                keys = slice(t * P, (t + 1) * P)
+                g, f = t // 2, t % 2
+                keys = slice((2 * f + g) * P, (2 * f + g + 1) * P)
                 nc.tensor.matmul_mx(
-                    out=bank_v[:, keys],
+                    out=bank_v[:, t * P : (t + 1) * P],
                     lhsT=x_codes_of[b][:, keys].bitcast(FP8X4),
                     lhsT_scale=x_scales_of[b][:, keys],
                     rhs=wv_codes[:, cols].bitcast(FP8X4),
@@ -132,7 +148,7 @@ def tile_relativeglobalattention_pa_t_kernel(tc, q, k, inputV, Wv, E, out):
                     start=True,
                     stop=True,
                 )
-            copy_out = nc.scalar.copy if (c % 2 == 1 and not live(b - 2)) else nc.vector.tensor_copy
+            copy_out = nc.scalar.copy if on_scalar else nc.vector.tensor_copy
             copy_out(
                 out=v_grouped_of[b][:, c * BANK : (c + 1) * BANK].rearrange("p (n t) -> p n t", t=PACK),
                 in_=bank_v[:].rearrange("p (t n) -> p n t", t=PACK),
@@ -158,9 +174,12 @@ def tile_relativeglobalattention_pa_t_kernel(tc, q, k, inputV, Wv, E, out):
                 )
             return bank
 
-        def relative_logits(b, a):
+        def relative_logits(b, a, vec=False):
             bank_qe = plain_logits(b, a, ET)
-            nc.scalar.mul(out=cats[b % N_CAT][:, a, 1 : 1 + L], in_=bank_qe[:], mul=INV_SQRT_DK)
+            if vec:
+                nc.vector.tensor_scalar_mul(out=cats[b % N_CAT][:, a, 1 : 1 + L], in0=bank_qe[:], scalar1=INV_SQRT_DK)
+            else:
+                nc.scalar.mul(out=cats[b % N_CAT][:, a, 1 : 1 + L], in_=bank_qe[:], mul=INV_SQRT_DK)
 
         def skew(b):
             flat = out[b].rearrange("l d -> (l d)")
@@ -209,25 +228,30 @@ def tile_relativeglobalattention_pa_t_kernel(tc, q, k, inputV, Wv, E, out):
             nc.vector.reciprocal(out=r_inv[:], in_=row_sum_of[b][:])
             r_inv_of[b] = r_inv
 
-        def turn_e(b):
-            e_grouped = work.tile([P, L * PACK], BF16, align_bytes=64)
-            grouped_words = e_grouped[:].bitcast(F32)
-            for h in range(2):
-                bank_e = turn_words(e_rows_of[b], range(4 * h, 4 * h + 4))
-                copy_out = nc.vector.tensor_copy if h == 0 else nc.scalar.copy
-                copy_out(
-                    out=grouped_words[:, h * BANK : (h + 1) * BANK].rearrange("p (a i u) -> p a i u", a=2, u=2),
-                    in_=bank_e[:].rearrange("p (a u i) -> p a i u", a=2, u=2),
-                )
-            e_grouped_of[b] = e_grouped
+        def turn_e(b, h, copy_out):
+            if h == 0:
+                e_grouped = work.tile([P, L * PACK], BF16, align_bytes=64)
+                e_grouped_of[b] = e_grouped
+            grouped_words = e_grouped_of[b][:].bitcast(F32)
+            bank_e = turn_words(e_rows_of[b], range(4 * h, 4 * h + 4))
+            copy_out(
+                out=grouped_words[:, h * BANK : (h + 1) * BANK].rearrange("p (a i u) -> p a i u", a=2, u=2),
+                in_=bank_e[:].rearrange("p (a u i) -> p a i u", a=2, u=2),
+            )
 
-        def quantise_e(b):
-            e_codes = work.tile([P, L], U32, align_bytes=64)
-            e_scales = work.tile([P, L], U8, align_bytes=64)
-            nc.vector.quantize_mx(out=e_codes[:].bitcast(FP8X4), scales=e_scales[:], in_=e_grouped_of[b][:])
-            e_codes_of[b], e_scales_of[b] = e_codes, e_scales
+        def quantise_e(b, first=0, last=TILES):
+            if first == 0:
+                e_codes = work.tile([P, L], U32, align_bytes=64)
+                e_scales = work.tile([P, L], U8, align_bytes=64)
+                e_codes_of[b], e_scales_of[b] = e_codes, e_scales
+            queries = slice(first * P, last * P)
+            nc.vector.quantize_mx(
+                out=e_codes_of[b][:, queries].bitcast(FP8X4),
+                scales=e_scales_of[b][:, queries],
+                in_=e_grouped_of[b][:, first * P * PACK : last * P * PACK],
+            )
 
-        def attend(b, n):
+        def attend(b, n, on_vector):
             if n == 0:
                 o_rows = work.tile([P, TILES * DV], F32)
                 o_rows_of[b] = o_rows
@@ -246,7 +270,7 @@ def tile_relativeglobalattention_pa_t_kernel(tc, q, k, inputV, Wv, E, out):
             )
             o_part = o_rows_of[b][:, a * DV + h * BANK : a * DV + (h + 1) * BANK]
             r_inv_a = r_inv_of[b][:, a : a + 1]
-            if n % 2 == 0 or live(b + 2):
+            if not on_vector:
                 nc.scalar.activation(out=o_part, in_=bank_o[:], func=COPY, scale=r_inv_a)
             else:
                 nc.vector.tensor_scalar_mul(out=o_part, in0=bank_o[:], scalar1=r_inv_a)
@@ -258,63 +282,144 @@ def tile_relativeglobalattention_pa_t_kernel(tc, q, k, inputV, Wv, E, out):
 
         e_table_rows = const.tile([P, TILES * DK], BF16)
         nc.sync.dma_start(out=e_table_rows[:], in_=E.rearrange("(p t) d -> p (t d)", t=TILES))
-        load_inputs(0)
-        wv_rows = const.tile([P, PACK * DV], BF16)
-        nc.sync.dma_start(
-            out=wv_rows[:].rearrange("w (u x) -> w u x", u=2),
-            in_=Wv.rearrange("(u w e) n -> w u (e n)", u=2, e=2),
-        )
-        for b in range(1, LOADS_AHEAD):
-            load_inputs(b)
+        load_q(0)
+        wv_halves = []
+        for h in range(2):
+            wv_rows = const.tile([P, PACK * BANK], BF16, name="wv_rows%d" % h)
+            cols = slice(h * BANK, (h + 1) * BANK)
+            for u in range(2):
+                nc.sync.dma_start(
+                    out=wv_rows[:].rearrange("w (u e n) -> w u e n", u=2, e=2)[:, u, :, :],
+                    in_=Wv.rearrange("(u w e) n -> u w e n", u=2, e=2)[u, :, :, cols],
+                )
+            wv_halves.append(wv_rows)
+            if h == 0:
+                load_x(0)
+        load_q(1)
+        load_k(0)
+        load_x(1)
+        load_k(1)
         ET = const.tile([P, L], F32)
         turn_interleaved_rows(e_table_rows, ET)
         wv_grouped = const.tile([P, DV * PACK], BF16, align_bytes=64)
-        nc.vector.tensor_copy(
-            out=wv_grouped[:].rearrange("w (n t) -> w n t", t=PACK),
-            in_=wv_rows[:].rearrange("w (t n) -> w n t", t=PACK),
-        )
         wv_codes = const.tile([P, DV], U32, align_bytes=64)
         wv_scales = const.tile([P, DV], U8, align_bytes=64)
-        nc.vector.quantize_mx(out=wv_codes[:].bitcast(FP8X4), scales=wv_scales[:], in_=wv_grouped[:])
 
-        for i in range(-AHEAD, B + 1):
-            if live(i + AHEAD + LOADS_AHEAD):
-                load_inputs(i + AHEAD + LOADS_AHEAD)
+        def group_weights(h, copy_out):
+            cols = slice(h * BANK, (h + 1) * BANK)
+            copy_out(
+                out=wv_grouped[:].rearrange("w (n t) -> w n t", t=PACK)[:, cols, :],
+                in_=wv_halves[h][:].rearrange("w (t n) -> w n t", t=PACK),
+            )
 
-            if live(i + 1):
-                new_values(i + 1)
+        def quantise_weights(h):
+            cols = slice(h * BANK, (h + 1) * BANK)
+            nc.vector.quantize_mx(
+                out=wv_codes[:, cols].bitcast(FP8X4),
+                scales=wv_scales[:, cols],
+                in_=wv_grouped[:, h * BANK * PACK : (h + 1) * BANK * PACK],
+            )
+
+        VC, SC = nc.vector.tensor_copy, nc.scalar.copy
+        turn_q(0, VC)
+        group_weights(0, VC)
+        for a in range(TILES):
+            relative_logits(0, a, a == 1)
+        skew(0)
+        load_inputs(2)
+        turn_x(0, (VC, SC))
+        quantise_weights(0)
+        turn_k(0)
+        turn_q(1)
+        quantise_x(0)
+        group_weights(1, VC)
+        new_values(0)
+        project_values(0, 0, False)
+        project_values(0, 1, True)
+        quantise_weights(1)
+        relative_logits(1, 0, False)
+        project_values(0, 2, False)
+        project_values(0, 3, False)
+        relative_logits(1, 1, False)
+        turn_x(1, (VC, SC))
+        quantise_v(0, 0)
+        project_values(0, 4, False)
+        relative_logits(1, 2, False)
+        project_values(0, 5, False)
+        quantise_x(1)
+        project_values(0, 6, False)
+        relative_logits(1, 3, False)
+        project_values(0, 7, True)
+        skew(1)
+        turn_k(1)
+        quantise_v(0, 1)
+        for i in range(-1, B - 2):
+            bA, bC, bD, bE, bF = i + 3, i + 2, i + 1, i, i - 1
+            if live(bA + 1):
+                load_inputs(bA + 1)
+            if live(bC):
+                new_values(bC)
             for n in range(BANKS):
-                if live(i + 1):
-                    project_values(i + 1, n)
+                if live(bC):
+                    project_values(bC, n, not live(bF) and n % 2 == 1)
                     if n == BANKS // 2 + 1:
-                        quantise_v(i + 1, 0)
-                if live(i - 1):
-                    attend(i - 1, n)
-            if live(i + 2):
-                quantise_x(i + 2)
-            if live(i + 1):
-                quantise_v(i + 1, 1)
+                        quantise_v(bC, 0)
+                if live(bF):
+                    attend(bF, n, False)
 
-            if live(i + AHEAD):
-                turn_q(i + AHEAD)
-            if live(i):
-                turn_e(i)
-            if live(i + AHEAD):
-                turn_kx(i + AHEAD)
+            if live(bA):
+                turn_q(bA)
+            if live(bE):
+                turn_e(bE, 0, VC)
+                turn_e(bE, 1, SC)
+            if live(bC):
+                quantise_v(bC, 1)
+            if live(bE):
+                quantise_e(bE)
+                invert_row_sums(bE)
+            if live(bA):
+                turn_x(bA)
+                turn_k(bA)
 
-            if live(i + 1):
-                new_softmax(i + 1)
+            if live(bD):
+                new_softmax(bD)
             for step in range(TILES + 1):
-                if live(i + 1) and step < TILES:
-                    add_logits(i + 1, step)
-                if live(i + 1) and step > 0:
-                    row_max(i + 1, step - 1)
-                if live(i + AHEAD) and step > 0:
-                    relative_logits(i + AHEAD, step - 1)
-                if live(i + 1) and step > 0:
-                    exponentials(i + 1, step - 1)
-                if live(i) and step == 1:
-                    invert_row_sums(i)
-                    quantise_e(i)
-            if live(i + AHEAD):
-                skew(i + AHEAD)
+                if live(bD) and step < TILES:
+                    add_logits(bD, step)
+                if live(bA) and step == 0:
+                    quantise_x(bA)
+                if live(bD) and 0 < step <= TILES:
+                    row_max(bD, step - 1)
+                if live(bA) and step < TILES:
+                    relative_logits(bA, step)
+                if not live(bA) and 0 < step <= TILES:
+                    attend(bE, step - 1, False)
+                if live(bD) and 0 < step <= TILES:
+                    exponentials(bD, step - 1)
+            if live(bA):
+                skew(bA)
+        y, z = B - 2, B - 1
+        for n in range(4, 8):
+            attend(y - 1, n, n % 2 == 0)
+        turn_e(y, 0, VC)
+        turn_e(y, 1, SC)
+        quantise_e(y)
+        invert_row_sums(y)
+        new_softmax(z)
+        for step in range(TILES + 1):
+            if step < TILES:
+                add_logits(z, step)
+            if step > 0:
+                row_max(z, step - 1)
+                attend(y, step - 1, False)
+                exponentials(z, step - 1)
+            if step == TILES - 1:
+                turn_e(z, 0, VC)
+        quantise_e(z, 0, 2)
+        for n in range(4, 8):
+            attend(y, n, n % 2 == 0)
+        turn_e(z, 1, SC)
+        invert_row_sums(z)
+        quantise_e(z, 2, 4)
+        for n in range(8):
+            attend(z, n, n % 2 == 0)

@@ -162,20 +162,20 @@ def tile_relativeglobalattention_pa_t_kernel(tc, q, k, inputV, Wv, E, out):
                 in_=v_grouped_of[b][:, h * BANK * PACK : (h + 1) * BANK * PACK],
             )
 
-        def plain_logits(b, a, keysT):
+        def plain_logits(b, a, columns):
             bank = psum.tile([P, BANK], F32, tag="bank")
             for e in range(2):
                 nc.tensor.matmul(
                     bank[:],
                     lhsT=pairs(qT_of[b])[:, a * P : (a + 1) * P, e],
-                    rhs=pairs(keysT)[:, :, e],
+                    rhs=columns(e),
                     start=(e == 0),
                     stop=(e == 1),
                 )
             return bank
 
         def relative_logits(b, a, vec=False):
-            bank_qe = plain_logits(b, a, ET)
+            bank_qe = plain_logits(b, a, lambda e: ET[:, e, :])
             if vec:
                 nc.vector.tensor_scalar_mul(out=cats[b % N_CAT][:, a, 1 : 1 + L], in0=bank_qe[:], scalar1=INV_SQRT_DK)
             else:
@@ -198,7 +198,7 @@ def tile_relativeglobalattention_pa_t_kernel(tc, q, k, inputV, Wv, E, out):
             e_rows_of[b], neg_max_of[b], row_sum_of[b] = e_rows, neg_max, row_sum
 
         def add_logits(b, a):
-            bank_qk = plain_logits(b, a, kT_of[b])
+            bank_qk = plain_logits(b, a, lambda e: pairs(kT_of[b])[:, :, e])
             s_a = s_of[b][:, a * L : (a + 1) * L]
             nc.vector.scalar_tensor_tensor(
                 out=s_a, in0=bank_qk[:], scalar=INV_SQRT_DK, in1=s_a, op0=MULT, op1=ADD
@@ -299,8 +299,12 @@ def tile_relativeglobalattention_pa_t_kernel(tc, q, k, inputV, Wv, E, out):
         load_k(0)
         load_x(1)
         load_k(1)
-        ET = const.tile([P, L], F32)
-        turn_interleaved_rows(e_table_rows, ET)
+        ET = const.tile([P, 2, L], BF16)
+        bank_ET = turn_words(e_table_rows, range(4))
+        nc.scalar.copy(
+            out=ET[:].rearrange("w e (p t) -> w e p t", t=4),
+            in_=bank_ET[:].bitcast(BF16).rearrange("w (t p e) -> w e p t", t=4, e=2),
+        )
         wv_grouped = const.tile([P, DV * PACK], BF16, align_bytes=64)
         wv_codes = const.tile([P, DV], U32, align_bytes=64)
         wv_scales = const.tile([P, DV], U8, align_bytes=64)

@@ -24,6 +24,7 @@ INV_SQRT_DK = 1.0 / 16.0
 BANKS = 8
 AHEAD = 3
 LOADS_AHEAD = 2
+WARM_UP = 5
 N_CAT = 2
 
 FLOPS = 2 * B * (L * D * DV + L * L * DV + 2 * L * L * DK)
@@ -51,6 +52,11 @@ def tile_relativeglobalattention_pa_t_kernel(tc, q, k, inputV, Wv, E, out):
 
         ident_f32 = const.tile([P, P], F32)
         masks.make_identity(nc, ident_f32[:])
+        idle = const.tile([P, BANK], BF16)
+        nc.vector.memset(idle[:], 0.0)
+        bank_idle = psum.tile([P, BANK], F32, tag="bank")
+        for n in range(WARM_UP):
+            nc.tensor.matmul(bank_idle[:], lhsT=idle[:, 0:P], rhs=idle[:], start=True, stop=True)
         warm = const.tile([P, 1], F32)
         nc.vector.memset(warm[:], 0.0)
         nc.scalar.activation(out=warm[:], in_=warm[:], func=EXP)

@@ -193,8 +193,11 @@ def tile_relativeglobalattention_pa_t_kernel(tc, q, k, inputV, Wv, E, out):
                 out=flat[0 : L * (L + 1)].rearrange("(p x) -> p x", p=P),
                 in_=cats[b % N_CAT][:].rearrange("p a c -> p (a c)"),
             )
+
+        def load_skewed(b):
+            flat = out[b].rearrange("l d -> (l d)")
             s = turned.tile([P, TILES * L], F32)
-            nc.gpsimd.dma_start(out=s[:], in_=flat[L : L + L * L].rearrange("(p x) -> p x", p=P))
+            nc.sync.dma_start(out=s[:], in_=flat[L : L + L * L].rearrange("(p x) -> p x", p=P))
             s_of[b] = s
 
         def new_softmax(b):
@@ -337,6 +340,7 @@ def tile_relativeglobalattention_pa_t_kernel(tc, q, k, inputV, Wv, E, out):
             relative_logits(0, a, a == 1)
         skew(0)
         load_inputs(2)
+        load_skewed(0)
         turn_x(0, (VC, SC))
         quantise_weights(0)
         turn_k(0)
@@ -376,6 +380,8 @@ def tile_relativeglobalattention_pa_t_kernel(tc, q, k, inputV, Wv, E, out):
                         quantise_v(bC, 0)
                 if live(bF):
                     attend(bF, n, False)
+                if n == 3 and live(bA - 1):
+                    load_skewed(bA - 1)
 
             if live(bA):
                 turn_q(bA)

@@ -181,7 +181,7 @@ def tile_relativeglobalattention_pa_t_kernel(tc, q, k, inputV, Wv, E, out):
             return bank
 
         def relative_logits(b, a, vec=False):
-            bank_qe = plain_logits(b, a, lambda e: ET[:, e, :])
+            bank_qe = plain_logits(b, a, lambda e: pairs(ET)[:, :, e])
             if vec:
                 nc.vector.tensor_scalar_mul(out=cats[b % N_CAT][:, a, 1 : 1 + L], in0=bank_qe[:], scalar1=INV_SQRT_DK)
             else:
@@ -308,22 +308,20 @@ def tile_relativeglobalattention_pa_t_kernel(tc, q, k, inputV, Wv, E, out):
         load_k(0)
         load_x(1)
         load_k(1)
-        ET = const.tile([P, 2, L], BF16)
-        bank_ET = turn_words(e_table_rows, range(4))
-        nc.scalar.copy(
-            out=ET[:].rearrange("w e (p t) -> w e p t", t=4),
-            in_=bank_ET[:].bitcast(BF16).rearrange("w (t p e) -> w e p t", t=4, e=2),
-        )
+        ET = const.tile([P, L], F32)
+        turn_interleaved_rows(e_table_rows, ET)
         wv_grouped = const.tile([P, DV * PACK], BF16, align_bytes=64)
         wv_codes = const.tile([P, DV], U32, align_bytes=64)
         wv_scales = const.tile([P, DV], U8, align_bytes=64)
 
-        def group_weights(h, copy_out):
+        def group_weights(h):
             cols = slice(h * BANK, (h + 1) * BANK)
-            copy_out(
-                out=wv_grouped[:].rearrange("w (n t) -> w n t", t=PACK)[:, cols, :],
-                in_=wv_halves[h][:].rearrange("w (t n) -> w n t", t=PACK),
-            )
+            grouped = wv_grouped[:].rearrange("w (n t) -> w n t", t=PACK)[:, cols, :]
+            rows_h = wv_halves[h][:].rearrange("w (t n) -> w n t", t=PACK)
+            if h == 0:
+                nc.vector.tensor_copy(out=grouped, in_=rows_h)
+            else:
+                nc.gpsimd.tensor_scalar(out=grouped, in0=rows_h, scalar1=1.0, scalar2=0.0, op0=MULT, op1=ADD)
 
         def quantise_weights(h):
             cols = slice(h * BANK, (h + 1) * BANK)
@@ -335,36 +333,38 @@ def tile_relativeglobalattention_pa_t_kernel(tc, q, k, inputV, Wv, E, out):
 
         VC, SC = nc.vector.tensor_copy, nc.scalar.copy
         turn_q(0, VC)
-        group_weights(0, VC)
-        for a in range(TILES):
+        group_weights(0)
+        group_weights(1)
+        for a in range(2):
             relative_logits(0, a, a == 1)
+        turn_x(0, (VC, SC))
+        for a in range(2, TILES):
+            relative_logits(0, a, False)
         skew(0)
         load_inputs(2)
         load_skewed(0)
-        turn_x(0, (VC, SC))
         quantise_weights(0)
-        turn_k(0)
-        turn_q(1)
         quantise_x(0)
-        group_weights(1, VC)
+        turn_q(1)
         new_values(0)
         project_values(0, 0, False)
-        project_values(0, 1, True)
         quantise_weights(1)
         relative_logits(1, 0, False)
+        project_values(0, 1, False)
         project_values(0, 2, False)
-        project_values(0, 3, False)
         relative_logits(1, 1, False)
+        project_values(0, 3, False)
         turn_x(1, (VC, SC))
-        quantise_v(0, 0)
         project_values(0, 4, False)
         relative_logits(1, 2, False)
+        quantise_v(0, 0)
         project_values(0, 5, False)
         quantise_x(1)
         project_values(0, 6, False)
         relative_logits(1, 3, False)
         project_values(0, 7, True)
         skew(1)
+        turn_k(0)
         turn_k(1)
         quantise_v(0, 1)
         for i in range(-1, B - 2):
@@ -391,8 +391,8 @@ def tile_relativeglobalattention_pa_t_kernel(tc, q, k, inputV, Wv, E, out):
             if live(bC):
                 quantise_v(bC, 1)
             if live(bE):
-                quantise_e(bE)
                 invert_row_sums(bE)
+                quantise_e(bE)
             if live(bA):
                 turn_x(bA)
                 turn_k(bA)
@@ -418,9 +418,10 @@ def tile_relativeglobalattention_pa_t_kernel(tc, q, k, inputV, Wv, E, out):
         for n in range(4, 8):
             attend(y - 1, n, n % 2 == 0)
         turn_e(y, 0, VC)
-        turn_e(y, 1, SC)
-        quantise_e(y)
+        turn_e(y, 1, VC)
         invert_row_sums(y)
+        quantise_e(y, 0, 2)
+        quantise_e(y, 2, 4)
         new_softmax(z)
         for step in range(TILES + 1):
             if step < TILES:

@@ -318,10 +318,7 @@ def tile_relativeglobalattention_pa_t_kernel(tc, q, k, inputV, Wv, E, out):
             cols = slice(h * BANK, (h + 1) * BANK)
             grouped = wv_grouped[:].rearrange("w (n t) -> w n t", t=PACK)[:, cols, :]
             rows_h = wv_halves[h][:].rearrange("w (t n) -> w n t", t=PACK)
-            if h == 0:
-                nc.vector.tensor_copy(out=grouped, in_=rows_h)
-            else:
-                nc.gpsimd.tensor_scalar(out=grouped, in0=rows_h, scalar1=1.0, scalar2=0.0, op0=MULT, op1=ADD)
+            nc.vector.tensor_copy(out=grouped, in_=rows_h)
 
         def quantise_weights(h):
             cols = slice(h * BANK, (h + 1) * BANK)
@@ -334,7 +331,6 @@ def tile_relativeglobalattention_pa_t_kernel(tc, q, k, inputV, Wv, E, out):
         VC, SC = nc.vector.tensor_copy, nc.scalar.copy
         turn_q(0, VC)
         group_weights(0)
-        group_weights(1)
         for a in range(2):
             relative_logits(0, a, a == 1)
         turn_x(0, (VC, SC))
@@ -347,18 +343,19 @@ def tile_relativeglobalattention_pa_t_kernel(tc, q, k, inputV, Wv, E, out):
         quantise_x(0)
         turn_q(1)
         new_values(0)
+        group_weights(1)
         project_values(0, 0, False)
-        quantise_weights(1)
         relative_logits(1, 0, False)
-        project_values(0, 1, False)
+        project_values(0, 1, True)
         project_values(0, 2, False)
+        quantise_weights(1)
         relative_logits(1, 1, False)
         project_values(0, 3, False)
         turn_x(1, (VC, SC))
         project_values(0, 4, False)
         relative_logits(1, 2, False)
         quantise_v(0, 0)
-        project_values(0, 5, False)
+        project_values(0, 5, True)
         quantise_x(1)
         project_values(0, 6, False)
         relative_logits(1, 3, False)

@@ -160,12 +160,12 @@ def tile_relativeglobalattention_pa_t_kernel(tc, q, k, inputV, Wv, E, out):
                 in_=bank_v[:].rearrange("p (t n) -> p n t", t=PACK),
             )
 
-        def quantise_v(b, h):
-            half = slice(h * BANK, (h + 1) * BANK)
+        def quantise_v(b, h, n=1):
+            half = slice(h * BANK, (h + n) * BANK)
             nc.vector.quantize_mx(
                 out=v_codes_of[b][:, half].bitcast(FP8X4),
                 scales=v_scales_of[b][:, half],
-                in_=v_grouped_of[b][:, h * BANK * PACK : (h + 1) * BANK * PACK],
+                in_=v_grouped_of[b][:, h * BANK * PACK : (h + n) * BANK * PACK],
             )
 
         def plain_logits(b, a, columns):
@@ -316,8 +316,8 @@ def tile_relativeglobalattention_pa_t_kernel(tc, q, k, inputV, Wv, E, out):
 
         def group_weights(h):
             cols = slice(h * BANK, (h + 1) * BANK)
-            grouped = wv_grouped[:].rearrange("w (n t) -> w n t", t=PACK)[:, cols, :]
-            rows_h = wv_halves[h][:].rearrange("w (t n) -> w n t", t=PACK)
+            grouped = wv_grouped[:].rearrange("w (n t) -> w n t", t=PACK)[:, cols, :].rearrange("w (c i) t -> w c t i", i=4)
+            rows_h = wv_halves[h][:].rearrange("w (t c i) -> w c t i", t=PACK, i=4)
             nc.vector.tensor_copy(out=grouped, in_=rows_h)
 
         def quantise_weights(h):
@@ -373,8 +373,6 @@ def tile_relativeglobalattention_pa_t_kernel(tc, q, k, inputV, Wv, E, out):
             for n in range(BANKS):
                 if live(bC):
                     project_values(bC, n, not live(bF) and n % 2 == 1)
-                    if n == BANKS // 2 + 1:
-                        quantise_v(bC, 0)
                 if live(bF):
                     attend(bF, n, False)
                 if n == 3 and live(bA - 1):
@@ -386,7 +384,7 @@ def tile_relativeglobalattention_pa_t_kernel(tc, q, k, inputV, Wv, E, out):
                 turn_e(bE, 0, VC)
                 turn_e(bE, 1, SC)
             if live(bC):
-                quantise_v(bC, 1)
+                quantise_v(bC, 0, 2)
             if live(bE):
                 invert_row_sums(bE)
                 quantise_e(bE)

@@ -341,7 +341,7 @@ def tile_relativeglobalattention_pa_t_kernel(tc, q, k, inputV, Wv, E, out):
         load_skewed(0)
         quantise_weights(0)
         quantise_x(0)
-        turn_q(1)
+        turn_q(1, VC)
         new_values(0)
         group_weights(1)
         project_values(0, 0, False)
@@ -362,7 +362,6 @@ def tile_relativeglobalattention_pa_t_kernel(tc, q, k, inputV, Wv, E, out):
         project_values(0, 7, True)
         skew(1)
         turn_k(0)
-        turn_k(1)
         quantise_v(0, 1)
         for i in range(-1, B - 2):
             bA, bC, bD, bE, bF = i + 3, i + 2, i + 1, i, i - 1
@@ -378,11 +377,11 @@ def tile_relativeglobalattention_pa_t_kernel(tc, q, k, inputV, Wv, E, out):
                 if n == 3 and live(bA - 1):
                     load_skewed(bA - 1)
 
-            if live(bA):
-                turn_q(bA)
             if live(bE):
                 turn_e(bE, 0, VC)
                 turn_e(bE, 1, SC)
+            if live(bA):
+                turn_q(bA)
             if live(bC):
                 quantise_v(bC, 0, 2)
             if live(bE):
@@ -391,6 +390,8 @@ def tile_relativeglobalattention_pa_t_kernel(tc, q, k, inputV, Wv, E, out):
             if live(bA):
                 turn_x(bA)
                 turn_k(bA)
+            if i == -1:
+                turn_k(1)
 
             if live(bD):
                 new_softmax(bD)
@@ -410,28 +411,29 @@ def tile_relativeglobalattention_pa_t_kernel(tc, q, k, inputV, Wv, E, out):
             if live(bA):
                 skew(bA)
         y, z = B - 2, B - 1
-        for n in range(4, 8):
-            attend(y - 1, n, n % 2 == 0)
-        turn_e(y, 0, VC)
-        turn_e(y, 1, VC)
-        invert_row_sums(y)
-        quantise_e(y, 0, 2)
-        quantise_e(y, 2, 4)
         new_softmax(z)
         for step in range(TILES + 1):
             if step < TILES:
                 add_logits(z, step)
             if step > 0:
                 row_max(z, step - 1)
-                attend(y, step - 1, False)
+                attend(y - 1, 3 + step, False)
                 exponentials(z, step - 1)
-            if step == TILES - 1:
-                turn_e(z, 0, VC)
-        quantise_e(z, 0, 2)
-        for n in range(4, 8):
+            if step == 1:
+                turn_e(y, 0, SC)
+            if step == 2:
+                turn_e(y, 1, VC)
+                invert_row_sums(y)
+            if step == 3:
+                quantise_e(y)
+        for n in range(BANKS):
             attend(y, n, n % 2 == 0)
-        turn_e(z, 1, SC)
-        invert_row_sums(z)
-        quantise_e(z, 2, 4)
-        for n in range(8):
+            if n == 1:
+                turn_e(z, 0, VC)
+            if n == 2:
+                turn_e(z, 1, SC)
+                invert_row_sums(z)
+            if n == 5:
+                quantise_e(z)
+        for n in range(BANKS):
             attend(z, n, n % 2 == 0)

from contextlib import ExitStack

import concourse.masks as masks
import concourse.mybir as mybir

F32 = mybir.dt.float32
BF16 = mybir.dt.bfloat16
U32 = mybir.dt.uint32
U8 = mybir.dt.uint8
FP8X4 = mybir.dt.float8_e4m3fn_x4
ADD = mybir.AluOpType.add
MULT = mybir.AluOpType.mult
MAX = mybir.AluOpType.max
EXP = mybir.ActivationFunctionType.Exp
COPY = mybir.ActivationFunctionType.Copy
FREE_AXIS = mybir.AxisListType.X

B, L, D, DK, DV = 8, 512, 512, 256, 1024
P = 128
TILES = L // P
BANK = 512
PACK = 4
INV_SQRT_DK = 1.0 / 16.0
BANKS = 8
AHEAD = 3
LOADS_AHEAD = 2
WARM_UP = 5
N_CAT = 2

FLOPS = 2 * B * (L * D * DV + L * L * DV + 2 * L * L * DK)


def pairs(words):
    return words[:].bitcast(BF16).rearrange("w (c e) -> w c e", e=2)


def tile_relativeglobalattention_pa_t_kernel(tc, q, k, inputV, Wv, E, out):
    nc = tc.nc
    with ExitStack() as ctx:
        ctx.enter_context(tc.manual_schedule())
        const = ctx.enter_context(tc.tile_pool(name="const", bufs=1))
        rows = ctx.enter_context(tc.tile_pool(name="rows", bufs=LOADS_AHEAD + 2))
        turned = ctx.enter_context(tc.tile_pool(name="turned", bufs=AHEAD))
        work = ctx.enter_context(tc.tile_pool(name="work", bufs=2))
        psum = ctx.enter_context(tc.psum_pool(name="psum", bufs=BANKS))

        q_rows_of, k_rows_of, x_rows_of = {}, {}, {}
        qT_of, kT_of, x_grouped_of, x_codes_of, x_scales_of = {}, {}, {}, {}, {}
        v_grouped_of, v_codes_of, v_scales_of = {}, {}, {}
        s_of, e_rows_of, neg_max_of, row_sum_of, r_inv_of = {}, {}, {}, {}, {}
        e_grouped_of, e_codes_of, e_scales_of, o_rows_of = {}, {}, {}, {}

        ident_f32 = const.tile([P, P], F32)
        masks.make_identity(nc, ident_f32[:])
        idle = const.tile([P, BANK], BF16)
        nc.vector.memset(idle[:], 0.0)
        bank_idle = psum.tile([P, BANK], F32, tag="bank")
        for n in range(WARM_UP):
            nc.tensor.matmul(bank_idle[:], lhsT=idle[:, 0:P], rhs=idle[:], start=True, stop=True)
        warm = const.tile([P, 1], F32)
        nc.vector.memset(warm[:], 0.0)
        nc.scalar.activation(out=warm[:], in_=warm[:], func=EXP)
        zeros = const.tile([P, TILES, 1], F32)
        nc.vector.memset(zeros[:], 0.0)
        cats = [const.tile([P, TILES, 1 + L], F32, name="cat%d" % n) for n in range(N_CAT)]
        for cat in cats:
            nc.scalar.copy(out=cat[:, :, 0:1], in_=zeros[:])

        def live(b):
            return 0 <= b < B

        def load_q(b):
            q_rows = rows.tile([P, TILES * DK], BF16)
            nc.sync.dma_start(out=q_rows[:], in_=q[b].rearrange("(p a) d -> p (a d)", a=TILES))
            q_rows_of[b] = q_rows

        def load_k(b):
            k_rows = rows.tile([P, TILES * DK], BF16)
            nc.sync.dma_start(out=k_rows[:], in_=k[b].rearrange("(p t) d -> p (t d)", t=TILES))
            k_rows_of[b] = k_rows

        def load_x(b):
            x_rows = rows.tile([P, TILES * D], BF16)
            nc.sync.dma_start(out=x_rows[:], in_=inputV[b].rearrange("(m t) d -> m (t d)", t=TILES))
            x_rows_of[b] = x_rows

        def load_inputs(b):
            load_q(b)
            load_x(b)
            load_k(b)

        def turn_words(src_rows, blocks):
            words = src_rows[:].bitcast(F32)
            bank = psum.tile([P, BANK], F32, tag="bank")
            for n, block in enumerate(blocks):
                nc.tensor.transpose(
                    bank[:, n * P : (n + 1) * P], words[:, block * P : (block + 1) * P], ident_f32[:]
                )
            return bank

        def turn_interleaved_rows(src_rows, dst_words, copy_out=nc.scalar.copy):
            bank = turn_words(src_rows, range(4))
            copy_out(
                out=dst_words[:].rearrange("w (p t) -> w p t", t=4),
                in_=bank[:].rearrange("w (t p) -> w p t", t=4),
            )

        def turn_q(b, copy_out=nc.scalar.copy):
            qT = turned.tile([P, L], F32)
            bank_q = turn_words(q_rows_of[b], range(4))
            copy_out(out=qT[:], in_=bank_q[:])
            qT_of[b] = qT

        def turn_k(b, copy_out=nc.scalar.copy):
            kT = turned.tile([P, L], F32)
            turn_interleaved_rows(k_rows_of[b], kT, copy_out)
            kT_of[b] = kT

        def turn_x(b, copies=None):
            x_grouped = work.tile([P, L * PACK], BF16, align_bytes=64)
            grouped_words = x_grouped[:].bitcast(F32).rearrange("w (f g m x) -> w f g m x", f=2, g=2, x=4)
            for f in range(2):
                bank_x = turn_words(x_rows_of[b], [2 * (2 * s + f) + u for s in range(2) for u in range(2)])
                copy_out = copies[f] if copies else nc.scalar.copy
                copy_out(
                    out=grouped_words[:, f, :, :, :], in_=bank_x[:].rearrange("w (x g m) -> w g m x", x=4, g=2)
                )
            x_grouped_of[b] = x_grouped

        def quantise_x(b):
            x_codes = work.tile([P, L], U32, align_bytes=64)
            x_scales = work.tile([P, L], U8, align_bytes=64)
            nc.vector.quantize_mx(out=x_codes[:].bitcast(FP8X4), scales=x_scales[:], in_=x_grouped_of[b][:])
            x_codes_of[b], x_scales_of[b] = x_codes, x_scales

        def new_values(b):
            v_grouped = work.tile([P, DV * PACK], BF16, align_bytes=64)
            v_codes = work.tile([P, DV], U32, align_bytes=64, bufs=4)
            v_scales = work.tile([P, DV], U8, align_bytes=64, bufs=4)
            v_grouped_of[b], v_codes_of[b], v_scales_of[b] = v_grouped, v_codes, v_scales

        def project_values(b, c, on_scalar):
            cols = slice(c * P, (c + 1) * P)
            bank_v = psum.tile([P, BANK], F32, tag="bank")
            for t in range(TILES):
                g, f = t // 2, t % 2
                keys = slice((2 * f + g) * P, (2 * f + g + 1) * P)
                nc.tensor.matmul_mx(
                    out=bank_v[:, t * P : (t + 1) * P],
                    lhsT=x_codes_of[b][:, keys].bitcast(FP8X4),
                    lhsT_scale=x_scales_of[b][:, keys],
                    rhs=wv_codes[:, cols].bitcast(FP8X4),
                    rhs_scale=wv_scales[:, cols],
                    start=True,
                    stop=True,
                )
            copy_out = nc.scalar.copy if on_scalar else nc.vector.tensor_copy
            copy_out(
                out=v_grouped_of[b][:, c * BANK : (c + 1) * BANK].rearrange("p (n t) -> p n t", t=PACK),
                in_=bank_v[:].rearrange("p (t n) -> p n t", t=PACK),
            )

        def quantise_v(b, h, n=1):
            half = slice(h * BANK, (h + n) * BANK)
            nc.vector.quantize_mx(
                out=v_codes_of[b][:, half].bitcast(FP8X4),
                scales=v_scales_of[b][:, half],
                in_=v_grouped_of[b][:, h * BANK * PACK : (h + n) * BANK * PACK],
            )

        def plain_logits(b, a, columns):
            bank = psum.tile([P, BANK], F32, tag="bank")
            for e in range(2):
                nc.tensor.matmul(
                    bank[:],
                    lhsT=pairs(qT_of[b])[:, a * P : (a + 1) * P, e],
                    rhs=columns(e),
                    start=(e == 0),
                    stop=(e == 1),
                )
            return bank

        def relative_logits(b, a, vec=False):
            bank_qe = plain_logits(b, a, lambda e: pairs(ET)[:, :, e])
            if vec:
                nc.vector.tensor_scalar_mul(out=cats[b % N_CAT][:, a, 1 : 1 + L], in0=bank_qe[:], scalar1=INV_SQRT_DK)
            else:
                nc.scalar.mul(out=cats[b % N_CAT][:, a, 1 : 1 + L], in_=bank_qe[:], mul=INV_SQRT_DK)

        def skew(b):
            flat = out[b].rearrange("l d -> (l d)")
            nc.sync.dma_start(
                out=flat[0 : L * (L + 1)].rearrange("(p x) -> p x", p=P),
                in_=cats[b % N_CAT][:].rearrange("p a c -> p (a c)"),
            )

        def load_skewed(b):
            flat = out[b].rearrange("l d -> (l d)")
            s = turned.tile([P, TILES * L], F32)
            nc.sync.dma_start(out=s[:], in_=flat[L : L + L * L].rearrange("(p x) -> p x", p=P))
            s_of[b] = s

        def new_softmax(b):
            e_rows = work.tile([P, TILES * L], BF16)
            neg_max = work.tile([P, TILES], F32)
            row_sum = work.tile([P, TILES], F32)
            e_rows_of[b], neg_max_of[b], row_sum_of[b] = e_rows, neg_max, row_sum

        def add_logits(b, a):
            bank_qk = plain_logits(b, a, lambda e: pairs(kT_of[b])[:, :, e])
            s_a = s_of[b][:, a * L : (a + 1) * L]
            nc.vector.scalar_tensor_tensor(
                out=s_a, in0=bank_qk[:], scalar=INV_SQRT_DK, in1=s_a, op0=MULT, op1=ADD
            )

        def row_max(b, a):
            nc.vector.tensor_reduce(
                out=neg_max_of[b][:, a : a + 1],
                in_=s_of[b][:, a * L : (a + 1) * L],
                axis=FREE_AXIS,
                op=MAX,
                negate=True,
            )

        def exponentials(b, a):
            nc.scalar.activation(
                out=e_rows_of[b][:, a * L : (a + 1) * L],
                in_=s_of[b][:, a * L : (a + 1) * L],
                func=EXP,
                bias=neg_max_of[b][:, a : a + 1],
                scale=1.0,
                accum_out=row_sum_of[b][:, a : a + 1],
            )

        def invert_row_sums(b):
            r_inv = work.tile([P, TILES], F32)
            nc.vector.reciprocal(out=r_inv[:], in_=row_sum_of[b][:])
            r_inv_of[b] = r_inv

        def turn_e(b, h, copy_out):
            if h == 0:
                e_grouped = work.tile([P, L * PACK], BF16, align_bytes=64)
                e_grouped_of[b] = e_grouped
            grouped_words = e_grouped_of[b][:].bitcast(F32)
            bank_e = turn_words(e_rows_of[b], range(4 * h, 4 * h + 4))
            copy_out(
                out=grouped_words[:, h * BANK : (h + 1) * BANK].rearrange("p (a i u) -> p a i u", a=2, u=2),
                in_=bank_e[:].rearrange("p (a u i) -> p a i u", a=2, u=2),
            )

        def quantise_e(b, first=0, last=TILES):
            if first == 0:
                e_codes = work.tile([P, L], U32, align_bytes=64)
                e_scales = work.tile([P, L], U8, align_bytes=64)
                e_codes_of[b], e_scales_of[b] = e_codes, e_scales
            queries = slice(first * P, last * P)
            nc.vector.quantize_mx(
                out=e_codes_of[b][:, queries].bitcast(FP8X4),
                scales=e_scales_of[b][:, queries],
                in_=e_grouped_of[b][:, first * P * PACK : last * P * PACK],
            )

        def attend(b, n, on_vector):
            if n == 0:
                o_rows = work.tile([P, TILES * DV], F32)
                o_rows_of[b] = o_rows
            a, h = n // 2, n % 2
            queries = slice(a * P, (a + 1) * P)
            half = slice(h * BANK, (h + 1) * BANK)
            bank_o = psum.tile([P, BANK], F32, tag="bank")
            nc.tensor.matmul_mx(
                out=bank_o[:],
                lhsT=e_codes_of[b][:, queries].bitcast(FP8X4),
                lhsT_scale=e_scales_of[b][:, queries],
                rhs=v_codes_of[b][:, half].bitcast(FP8X4),
                rhs_scale=v_scales_of[b][:, half],
                start=True,
                stop=True,
            )
            o_part = o_rows_of[b][:, a * DV + h * BANK : a * DV + (h + 1) * BANK]
            r_inv_a = r_inv_of[b][:, a : a + 1]
            if not on_vector:
                nc.scalar.activation(out=o_part, in_=bank_o[:], func=COPY, scale=r_inv_a)
            else:
                nc.vector.tensor_scalar_mul(out=o_part, in0=bank_o[:], scalar1=r_inv_a)
            if h == 1:
                part = slice(a * DV, (a + 1) * DV)
                nc.sync.dma_start(
                    out=out[b].rearrange("(p a) d -> p (a d)", a=TILES)[:, part], in_=o_rows_of[b][:, part]
                )

        e_table_rows = const.tile([P, TILES * DK], BF16)
        nc.sync.dma_start(out=e_table_rows[:], in_=E.rearrange("(p t) d -> p (t d)", t=TILES))
        load_q(0)
        wv_halves = []
        for h in range(2):
            wv_rows = const.tile([P, PACK * BANK], BF16, name="wv_rows%d" % h)
            cols = slice(h * BANK, (h + 1) * BANK)
            for u in range(2):
                nc.sync.dma_start(
                    out=wv_rows[:].rearrange("w (u e n) -> w u e n", u=2, e=2)[:, u, :, :],
                    in_=Wv.rearrange("(u w e) n -> u w e n", u=2, e=2)[u, :, :, cols],
                )
            wv_halves.append(wv_rows)
            if h == 0:
                load_x(0)
        load_q(1)
        load_k(0)
        load_x(1)
        load_k(1)
        ET = const.tile([P, L], F32)
        turn_interleaved_rows(e_table_rows, ET)
        wv_grouped = const.tile([P, DV * PACK], BF16, align_bytes=64)
        wv_codes = const.tile([P, DV], U32, align_bytes=64)
        wv_scales = const.tile([P, DV], U8, align_bytes=64)

        def group_weights(h):
            cols = slice(h * BANK, (h + 1) * BANK)
            grouped = wv_grouped[:].rearrange("w (n t) -> w n t", t=PACK)[:, cols, :].rearrange("w (c i) t -> w c t i", i=4)
            rows_h = wv_halves[h][:].rearrange("w (t c i) -> w c t i", t=PACK, i=4)
            nc.vector.tensor_copy(out=grouped, in_=rows_h)

        def quantise_weights(h):
            cols = slice(h * BANK, (h + 1) * BANK)
            nc.vector.quantize_mx(
                out=wv_codes[:, cols].bitcast(FP8X4),
                scales=wv_scales[:, cols],
                in_=wv_grouped[:, h * BANK * PACK : (h + 1) * BANK * PACK],
            )

        VC, SC = nc.vector.tensor_copy, nc.scalar.copy
        turn_q(0, VC)
        group_weights(0)
        for a in range(2):
            relative_logits(0, a, a == 1)
        turn_x(0, (VC, SC))
        for a in range(2, TILES):
            relative_logits(0, a, False)
        skew(0)
        load_inputs(2)
        load_skewed(0)
        quantise_weights(0)
        quantise_x(0)
        turn_q(1, VC)
        new_values(0)
        group_weights(1)
        project_values(0, 0, False)
        relative_logits(1, 0, False)
        project_values(0, 1, True)
        project_values(0, 2, False)
        quantise_weights(1)
        relative_logits(1, 1, False)
        project_values(0, 3, False)
        turn_x(1, (VC, SC))
        project_values(0, 4, False)
        relative_logits(1, 2, False)
        quantise_v(0, 0)
        project_values(0, 5, True)
        quantise_x(1)
        project_values(0, 6, False)
        relative_logits(1, 3, False)
        project_values(0, 7, True)
        skew(1)
        turn_k(0)
        quantise_v(0, 1)
        for i in range(-1, B - 2):
            bA, bC, bD, bE, bF = i + 3, i + 2, i + 1, i, i - 1
            if live(bA + 1):
                load_inputs(bA + 1)
            if live(bC):
                new_values(bC)
            for n in range(BANKS):
                if live(bC):
                    project_values(bC, n, not live(bF) and n % 2 == 1)
                if live(bF):
                    attend(bF, n, False)
                if n == 3 and live(bA - 1):
                    load_skewed(bA - 1)

            if live(bE):
                turn_e(bE, 0, VC)
                turn_e(bE, 1, SC)
            if live(bA):
                turn_q(bA)
            if live(bC):
                quantise_v(bC, 0, 2)
            if live(bE):
                invert_row_sums(bE)
                quantise_e(bE)
            if live(bA):
                turn_x(bA)
                turn_k(bA)
            if i == -1:
                turn_k(1)

            if live(bD):
                new_softmax(bD)
            for step in range(TILES + 1):
                if live(bD) and step < TILES:
                    add_logits(bD, step)
                if live(bA) and step == 0:
                    quantise_x(bA)
                if live(bD) and 0 < step <= TILES:
                    row_max(bD, step - 1)
                if live(bA) and step < TILES:
                    relative_logits(bA, step)
                if not live(bA) and 0 < step <= TILES:
                    attend(bE, step - 1, False)
                if live(bD) and 0 < step <= TILES:
                    exponentials(bD, step - 1)
            if live(bA):
                skew(bA)
        y, z = B - 2, B - 1
        new_softmax(z)
        for step in range(TILES + 1):
            if step < TILES:
                add_logits(z, step)
            if step > 0:
                row_max(z, step - 1)
                attend(y - 1, 3 + step, False)
                exponentials(z, step - 1)
            if step == 1:
                turn_e(y, 0, SC)
            if step == 2:
                turn_e(y, 1, VC)
                invert_row_sums(y)
            if step == 3:
                quantise_e(y)
        for n in range(BANKS):
            attend(y, n, n % 2 == 0)
            if n == 1:
                turn_e(z, 0, VC)
            if n == 2:
                turn_e(z, 1, SC)
                invert_row_sums(z)
            if n == 5:
                quantise_e(z)
        for n in range(BANKS):
            attend(z, n, n % 2 == 0)
